import numpy as np
import ml_dtypes


def mxq(x, axis, fmt="e4m3"):
    dtype, down = {"e4m3": (ml_dtypes.float8_e4m3fn, 7), "e5m2": (ml_dtypes.float8_e5m2, 14)}[fmt]
    v = np.moveaxis(np.asarray(x, np.float32).astype(ml_dtypes.bfloat16).astype(np.float64), axis, -1)
    blocks = v.reshape(v.shape[:-1] + (-1, 32))
    amax = np.abs(blocks).max(-1, keepdims=True)
    byte = np.maximum(np.where(amax > 0, np.frexp(amax)[1] - 1 + 127, 0) - down, 1)
    scale = np.exp2(byte - 127.0)
    codes = (blocks / scale).astype(np.float32).astype(dtype).astype(np.float64)
    return np.moveaxis((codes * scale).reshape(v.shape), -1, axis)


WIDE = False


def mx_kscale(k):
    if not WIDE:
        return np.ones(k)
    levels = np.array([10, -10, 5, -5, 0])
    a = np.random.permutation(np.resize(levels, k // 512 * 4)).reshape(k // 512, 4)
    idx = np.arange(k)
    return np.exp2(a[idx // 512, idx % 128 // 32])


BF16 = ml_dtypes.bfloat16


def bf(x):
    return np.asarray(x, np.float32).astype(BF16)


def f64(x):
    return np.asarray(x).astype(np.float64)


T, K, D = 16384, 512, 128
ACTIVE = 128.0


def setup_inputs():
    s = mx_kscale(K)
    allow = s <= max(s.min(), s.max() * 2.0 ** -18)
    p = np.maximum(np.random.uniform(-0.15, 1.0, (T, 1)), 0.0) * ACTIVE / K
    on = (np.random.uniform(size=(T, K)) < p) & allow[None, :]
    flags = 0.5 * np.random.uniform(size=(T, K)) + 0.5 * on
    w = np.random.standard_normal((K, D)) * (s / s.min())[:, None]
    return {"flags_matrix": bf(flags), "emb_weight": bf(w)}


def reference(flags_matrix, emb_weight):
    mask = (f64(flags_matrix) > 0.5).astype(np.float64)
    counts = np.sum(mask, axis=1, keepdims=True)
    sums = mxq(mask, 1, "e4m3") @ mxq(f64(emb_weight), 0, "e4m3")
    return np.where(counts > 0, sums / np.maximum(counts, 1.0), 0.0)

@@ -1,0 +1,159 @@
+from contextlib import ExitStack
+
+import concourse.mybir as mybir
+from concourse.masks import make_identity
+
+T, K, D = 16384, 512, 128
+FLOPS = 2 * T * K * D
+
+P = 128
+NT = T // P
+TPC = 8
+NCH = NT // TPC
+
+BF16 = mybir.dt.bfloat16
+F32 = mybir.dt.float32
+U32 = mybir.dt.uint32
+U8 = mybir.dt.uint8
+FP8X4 = mybir.dt.float8_e4m3fn_x4
+ALU = mybir.AluOpType
+ACT = mybir.ActivationFunctionType
+
+
+def tile_flagbagencoder_t_kernel(tc, flags_matrix, emb_weight, out):
+    nc = tc.nc
+    flags_v = flags_matrix.rearrange("(p j) k -> p j k", j=NT)
+    out_v = out.rearrange("(p j) d -> p j d", j=NT)
+
+    with ExitStack() as ctx:
+        const = ctx.enter_context(tc.tile_pool(name="const", bufs=1))
+        flp = ctx.enter_context(tc.tile_pool(name="flp", bufs=NCH))
+        gp = ctx.enter_context(tc.tile_pool(name="gp", bufs=3))
+        cp = ctx.enter_context(tc.tile_pool(name="cp", bufs=3))
+        op = ctx.enter_context(tc.tile_pool(name="op", bufs=4))
+        small = ctx.enter_context(tc.tile_pool(name="small", bufs=4))
+        psum = ctx.enter_context(tc.psum_pool(name="psum", bufs=1))
+        ctx.enter_context(tc.manual_schedule())
+
+        fl = {}
+        grouped = {}
+        codes = {}
+        scales = {}
+        sums = {}
+
+        w_raw = const.tile([P, 4, D], BF16, name="w_raw")
+        nc.scalar.dma_start(
+            out=w_raw[:].rearrange("p (u e) d -> p u e d", u=2),
+            in_=emb_weight.rearrange("(u p e) d -> p u e d", u=2, e=2),
+        )
+        for c in range(NCH):
+            fl[c] = flp.tile([P, TPC * K], BF16, name="fl", tag="fl")
+            view = fl[c][:].rearrange("p (j k) -> p j k", k=K)
+            pieces = 4 if c == 0 else 1
+            step = TPC // pieces
+            for s in range(pieces):
+                nc.sync.dma_start(
+                    out=view[:, s * step : (s + 1) * step, :],
+                    in_=flags_v[:, c * TPC + s * step : c * TPC + (s + 1) * step, :],
+                )
+
+        ident = const.tile([P, P], F32, name="ident")
+        make_identity(nc, ident[:])
+        cnt = const.tile([P, NT], F32, name="cnt")
+        rc = const.tile([P, NT], F32, name="rc")
+        w_grouped = const.tile([P, D, 4], BF16, name="w_grouped", align_bytes=64)
+        w_codes = const.tile([P, D], U32, name="w_codes", align_bytes=64)
+        w_scales = const.tile([P, D], U8, name="w_scales", align_bytes=64)
+
+        def weights():
+            nc.vector.tensor_copy(out=w_grouped[:], in_=w_raw[:].rearrange("p t d -> p d t"))
+            nc.vector.quantize_mx(
+                out=w_codes[:].bitcast(FP8X4),
+                scales=w_scales[:],
+                in_=w_grouped[:].rearrange("p d t -> p (d t)"),
+            )
+
+        def compare_count(c):
+            for j in range(TPC):
+                nc.vector.tensor_scalar(
+                    out=fl[c][:, j * K : (j + 1) * K],
+                    in0=fl[c][:, j * K : (j + 1) * K],
+                    scalar1=0.5,
+                    scalar2=None,
+                    op0=ALU.is_gt,
+                    op1=ALU.add,
+                    accum_out=cnt[:, c * TPC + j : c * TPC + j + 1],
+                )
+            cm = small.tile([P, TPC], F32, name="cm", tag="cm")
+            nc.vector.tensor_scalar_max(out=cm[:], in0=cnt[:, c * TPC : (c + 1) * TPC], scalar1=1.0)
+            nc.vector.reciprocal(out=rc[:, c * TPC : (c + 1) * TPC], in_=cm[:])
+
+        def transpose_evacuate(c):
+            words = fl[c][:].bitcast(F32)
+            grouped[c] = gp.tile([P, TPC * K], BF16, name="g", tag="g", align_bytes=64)
+            g_words = grouped[c][:].bitcast(F32)
+            for b in range(TPC // 2):
+                xt = psum.tile([P, 512], F32, name="xt%d" % b, tag="xt%d" % b)
+                for i in range(2):
+                    for u in range(2):
+                        col = (2 * b + i) * 256 + u * 128
+                        nc.tensor.transpose(
+                            out=xt[:, (2 * i + u) * 128 : (2 * i + u + 1) * 128],
+                            in_=words[:, col : col + 128],
+                            identity=ident[:],
+                        )
+                nc.scalar.copy(
+                    out=g_words[:, b * 512 : (b + 1) * 512].rearrange("p (i r u) -> p i r u", i=2, u=2),
+                    in_=xt[:].rearrange("p (i u r) -> p i r u", i=2, u=2),
+                )
+
+        def quantise(c):
+            codes[c] = cp.tile([P, TPC * P], U32, name="codes", tag="codes", align_bytes=64)
+            scales[c] = cp.tile([P, TPC * P], U8, name="scl", tag="scl", align_bytes=64)
+            nc.vector.quantize_mx(
+                out=codes[c][:].bitcast(FP8X4), scales=scales[c][:], in_=grouped[c][:]
+            )
+
+        def multiply(c):
+            sums[c] = []
+            for h in range(TPC // 4):
+                mo = psum.tile([P, 512], F32, name="mo%d" % h, tag="mo%d" % h, bufs=2)
+                sums[c].append(mo)
+                for q in range(4):
+                    j = 4 * h + q
+                    nc.tensor.matmul_mx(
+                        out=mo[:, q * D : (q + 1) * D],
+                        lhsT=codes[c][:, j * P : (j + 1) * P].bitcast(FP8X4),
+                        lhsT_scale=scales[c][:, j * P : (j + 1) * P],
+                        rhs=w_codes[:].bitcast(FP8X4),
+                        rhs_scale=w_scales[:],
+                        start=True,
+                        stop=True,
+                    )
+
+        def finish(c):
+            ot = op.tile([P, TPC * D], F32, name="ot", tag="ot")
+            for j in range(TPC):
+                nc.scalar.activation(
+                    out=ot[:, j * D : (j + 1) * D],
+                    in_=sums[c][j // 4][:, (j % 4) * D : (j % 4 + 1) * D],
+                    func=ACT.Copy,
+                    scale=rc[:, c * TPC + j : c * TPC + j + 1],
+                )
+            nc.gpsimd.dma_start(
+                out=out_v[:, c * TPC : (c + 1) * TPC, :],
+                in_=ot[:].rearrange("p (j d) -> p j d", d=D),
+            )
+
+        for k in range(NCH + 2):
+            if 0 <= k - 2:
+                quantise(k - 2)
+            if 0 <= k - 1 < NCH:
+                transpose_evacuate(k - 1)
+            if 0 <= k - 2:
+                multiply(k - 2)
+                finish(k - 2)
+            if k < NCH:
+                compare_count(k)
+            if k == 0:
+                weights()

@@ -10,6 +10,7 @@ P = 128
 NT = T // P
 TPC = 8
 NCH = NT // TPC
+PF = 8
 
 BF16 = mybir.dt.bfloat16
 F32 = mybir.dt.float32
@@ -30,7 +31,7 @@ def tile_flagbagencoder_t_kernel(tc, flags_matrix, emb_weight, out):
         flp = ctx.enter_context(tc.tile_pool(name="flp", bufs=NCH))
         gp = ctx.enter_context(tc.tile_pool(name="gp", bufs=3))
         cp = ctx.enter_context(tc.tile_pool(name="cp", bufs=3))
-        op = ctx.enter_context(tc.tile_pool(name="op", bufs=4))
+        op = ctx.enter_context(tc.tile_pool(name="op", bufs=6))
         small = ctx.enter_context(tc.tile_pool(name="small", bufs=4))
         psum = ctx.enter_context(tc.psum_pool(name="psum", bufs=1))
         ctx.enter_context(tc.manual_schedule())
@@ -46,7 +47,7 @@ def tile_flagbagencoder_t_kernel(tc, flags_matrix, emb_weight, out):
             out=w_raw[:].rearrange("p (u e) d -> p u e d", u=2),
             in_=emb_weight.rearrange("(u p e) d -> p u e d", u=2, e=2),
         )
-        for c in range(NCH):
+        def load(c):
             fl[c] = flp.tile([P, TPC * K], BF16, name="fl", tag="fl")
             view = fl[c][:].rearrange("p (j k) -> p j k", k=K)
             pieces = 4 if c == 0 else 1
@@ -56,6 +57,9 @@ def tile_flagbagencoder_t_kernel(tc, flags_matrix, emb_weight, out):
                     out=view[:, s * step : (s + 1) * step, :],
                     in_=flags_v[:, c * TPC + s * step : c * TPC + (s + 1) * step, :],
                 )
+
+        for c in range(PF):
+            load(c)
 
         ident = const.tile([P, P], F32, name="ident")
         make_identity(nc, ident[:])
@@ -140,12 +144,14 @@ def tile_flagbagencoder_t_kernel(tc, flags_matrix, emb_weight, out):
                     func=ACT.Copy,
                     scale=rc[:, c * TPC + j : c * TPC + j + 1],
                 )
-            nc.gpsimd.dma_start(
+            nc.sync.dma_start(
                 out=out_v[:, c * TPC : (c + 1) * TPC, :],
                 in_=ot[:].rearrange("p (j d) -> p j d", d=D),
             )
 
         for k in range(NCH + 2):
+            if k + PF < NCH:
+                load(k + PF)
             if 0 <= k - 2:
                 quantise(k - 2)
             if 0 <= k - 1 < NCH:

@@ -11,14 +11,18 @@ NT = T // P
 TPC = 8
 NCH = NT // TPC
 PF = 8
+NB = 4 * TPC
+NONES = 11
 
 BF16 = mybir.dt.bfloat16
 F32 = mybir.dt.float32
+I32 = mybir.dt.int32
 U32 = mybir.dt.uint32
 U8 = mybir.dt.uint8
 FP8X4 = mybir.dt.float8_e4m3fn_x4
 ALU = mybir.AluOpType
 ACT = mybir.ActivationFunctionType
+AX = mybir.AxisListType
 
 
 def tile_flagbagencoder_t_kernel(tc, flags_matrix, emb_weight, out):
@@ -41,18 +45,23 @@ def tile_flagbagencoder_t_kernel(tc, flags_matrix, emb_weight, out):
         codes = {}
         scales = {}
         sums = {}
+        partial = {}
+        partial_sb = {}
 
         w_raw = const.tile([P, 4, D], BF16, name="w_raw")
         nc.scalar.dma_start(
             out=w_raw[:].rearrange("p (u e) d -> p u e d", u=2),
             in_=emb_weight.rearrange("(u p e) d -> p u e d", u=2, e=2),
         )
+
+        def pieces_of(c):
+            return 4 if c == 0 else 1
+
         def load(c):
             fl[c] = flp.tile([P, TPC * K], BF16, name="fl", tag="fl")
             view = fl[c][:].rearrange("p (j k) -> p j k", k=K)
-            pieces = 4 if c == 0 else 1
-            step = TPC // pieces
-            for s in range(pieces):
+            step = TPC // pieces_of(c)
+            for s in range(pieces_of(c)):
                 nc.sync.dma_start(
                     out=view[:, s * step : (s + 1) * step, :],
                     in_=flags_v[:, c * TPC + s * step : c * TPC + (s + 1) * step, :],
@@ -63,34 +72,39 @@ def tile_flagbagencoder_t_kernel(tc, flags_matrix, emb_weight, out):
 
         ident = const.tile([P, P], F32, name="ident")
         make_identity(nc, ident[:])
-        cnt = const.tile([P, NT], F32, name="cnt")
         rc = const.tile([P, NT], F32, name="rc")
         w_grouped = const.tile([P, D, 4], BF16, name="w_grouped", align_bytes=64)
         w_codes = const.tile([P, D], U32, name="w_codes", align_bytes=64)
         w_scales = const.tile([P, D], U8, name="w_scales", align_bytes=64)
+        ones = const.tile([P, 16], BF16, name="ones")
+        fold = const.tile([P, 32], F32, name="fold")
+        sel = const.tile([P, 4 * P], BF16, name="sel")
 
-        def weights():
+        def constants():
+            nc.vector.memset(ones[:], 1.0)
             nc.vector.tensor_copy(out=w_grouped[:], in_=w_raw[:].rearrange("p t d -> p d t"))
             nc.vector.quantize_mx(
                 out=w_codes[:].bitcast(FP8X4),
                 scales=w_scales[:],
                 in_=w_grouped[:].rearrange("p d t -> p (d t)"),
             )
+            nc.vector.tensor_reduce(
+                out=fold[:], in_=ident[:].rearrange("p (l t) -> p l t", t=4), axis=AX.X, op=ALU.add
+            )
+            nc.vector.memset(sel[:].bitcast(I32), 0)
+            for h in range(4):
+                nc.vector.tensor_copy(out=sel[:, h * P + 32 * h : h * P + 32 * h + 32], in_=fold[:])
 
-        def compare_count(c):
-            for j in range(TPC):
+        def compare(c):
+            width = TPC * K // pieces_of(c)
+            for s in range(pieces_of(c)):
                 nc.vector.tensor_scalar(
-                    out=fl[c][:, j * K : (j + 1) * K],
-                    in0=fl[c][:, j * K : (j + 1) * K],
+                    out=fl[c][:, s * width : (s + 1) * width],
+                    in0=fl[c][:, s * width : (s + 1) * width],
                     scalar1=0.5,
                     scalar2=None,
                     op0=ALU.is_gt,
-                    op1=ALU.add,
-                    accum_out=cnt[:, c * TPC + j : c * TPC + j + 1],
                 )
-            cm = small.tile([P, TPC], F32, name="cm", tag="cm")
-            nc.vector.tensor_scalar_max(out=cm[:], in0=cnt[:, c * TPC : (c + 1) * TPC], scalar1=1.0)
-            nc.vector.reciprocal(out=rc[:, c * TPC : (c + 1) * TPC], in_=cm[:])
 
         def transpose_evacuate(c):
             words = fl[c][:].bitcast(F32)
@@ -111,6 +125,41 @@ def tile_flagbagencoder_t_kernel(tc, flags_matrix, emb_weight, out):
                     in_=xt[:].rearrange("p (i u r) -> p i r u", i=2, u=2),
                 )
 
+        def count_partial(c):
+            partial[c] = psum.tile([P, 512], F32, name="pc", tag="pc", bufs=2)
+            for j in range(TPC):
+                for h in range(4):
+                    col = (h * TPC + j) * NONES
+                    nc.tensor.matmul(
+                        out=partial[c][:, col : col + NONES],
+                        lhsT=grouped[c][:, (4 * j + h) * P : (4 * j + h + 1) * P],
+                        rhs=ones[:, 0:NONES],
+                        start=True,
+                        stop=True,
+                    )
+
+        def count_partial_out(c):
+            partial_sb[c] = small.tile([P, NB], BF16, name="p1", tag="p1")
+            nc.vector.tensor_copy(
+                out=partial_sb[c][:],
+                in_=partial[c][:, 0 : NB * NONES].rearrange("p (b n) -> p b n", n=NONES)[:, :, 0],
+            )
+
+        def count_total(c):
+            for h in range(4):
+                nc.tensor.matmul(
+                    out=partial[c][:, 504:512],
+                    lhsT=sel[:, h * P : (h + 1) * P],
+                    rhs=partial_sb[c][:, h * TPC : (h + 1) * TPC],
+                    start=(h == 0),
+                    stop=(h == 3),
+                )
+
+        def reciprocal(c):
+            cm = small.tile([P, TPC], F32, name="cm", tag="cm")
+            nc.vector.tensor_scalar_max(out=cm[:], in0=partial[c][:, 504:512], scalar1=1.0)
+            nc.vector.reciprocal(out=rc[:, c * TPC : (c + 1) * TPC], in_=cm[:])
+
         def quantise(c):
             codes[c] = cp.tile([P, TPC * P], U32, name="codes", tag="codes", align_bytes=64)
             scales[c] = cp.tile([P, TPC * P], U8, name="scl", tag="scl", align_bytes=64)
@@ -121,7 +170,7 @@ def tile_flagbagencoder_t_kernel(tc, flags_matrix, emb_weight, out):
         def multiply(c):
             sums[c] = []
             for h in range(TPC // 4):
-                mo = psum.tile([P, 512], F32, name="mo%d" % h, tag="mo%d" % h, bufs=2)
+                mo = psum.tile([P, 512], F32, name="mo%d" % h, tag="mo%d" % h)
                 sums[c].append(mo)
                 for q in range(4):
                     j = 4 * h + q
@@ -137,13 +186,19 @@ def tile_flagbagencoder_t_kernel(tc, flags_matrix, emb_weight, out):
 
         def finish(c):
             ot = op.tile([P, TPC * D], F32, name="ot", tag="ot")
-            for j in range(TPC):
+            for j in range(4):
                 nc.scalar.activation(
                     out=ot[:, j * D : (j + 1) * D],
-                    in_=sums[c][j // 4][:, (j % 4) * D : (j % 4 + 1) * D],
+                    in_=sums[c][0][:, j * D : (j + 1) * D],
                     func=ACT.Copy,
                     scale=rc[:, c * TPC + j : c * TPC + j + 1],
                 )
+            nc.vector.tensor_tensor(
+                out=ot[:, 4 * D : 8 * D].rearrange("p (q d) -> p q d", d=D),
+                in0=sums[c][1][:].rearrange("p (q d) -> p q d", d=D),
+                in1=rc[:, c * TPC + 4 : c * TPC + 8].unsqueeze(2).to_broadcast([P, 4, D]),
+                op=ALU.mult,
+            )
             nc.sync.dma_start(
                 out=out_v[:, c * TPC : (c + 1) * TPC, :],
                 in_=ot[:].rearrange("p (j d) -> p j d", d=D),
@@ -153,13 +208,19 @@ def tile_flagbagencoder_t_kernel(tc, flags_matrix, emb_weight, out):
             if k + PF < NCH:
                 load(k + PF)
             if 0 <= k - 2:
+                count_partial_out(k - 2)
                 quantise(k - 2)
             if 0 <= k - 1 < NCH:
                 transpose_evacuate(k - 1)
             if 0 <= k - 2:
+                count_total(k - 2)
                 multiply(k - 2)
-                finish(k - 2)
             if k < NCH:
-                compare_count(k)
+                compare(k)
             if k == 0:
-                weights()
+                constants()
+            if 0 <= k - 2:
+                reciprocal(k - 2)
+                finish(k - 2)
+            if 0 <= k - 1 < NCH:
+                count_partial(k - 1)

@@ -47,6 +47,7 @@ def tile_flagbagencoder_t_kernel(tc, flags_matrix, emb_weight, out):
         sums = {}
         partial = {}
         partial_sb = {}
+        xt = {}
 
         w_raw = const.tile([P, 4, D], BF16, name="w_raw")
         nc.scalar.dma_start(
@@ -79,6 +80,8 @@ def tile_flagbagencoder_t_kernel(tc, flags_matrix, emb_weight, out):
         ones = const.tile([P, 16], BF16, name="ones")
         fold = const.tile([P, 32], F32, name="fold")
         sel = const.tile([P, 4 * P], BF16, name="sel")
+        warm_in = const.tile([P, 8], F32, name="warm_in")
+        warm_out = const.tile([P, 8], F32, name="warm_out")
 
         def constants():
             nc.vector.memset(ones[:], 1.0)
@@ -106,28 +109,31 @@ def tile_flagbagencoder_t_kernel(tc, flags_matrix, emb_weight, out):
                     op0=ALU.is_gt,
                 )
 
-        def transpose_evacuate(c):
+        def transpose(c, b):
             words = fl[c][:].bitcast(F32)
-            grouped[c] = gp.tile([P, TPC * K], BF16, name="g", tag="g", align_bytes=64)
-            g_words = grouped[c][:].bitcast(F32)
-            for b in range(TPC // 2):
-                xt = psum.tile([P, 512], F32, name="xt%d" % b, tag="xt%d" % b)
-                for i in range(2):
-                    for u in range(2):
-                        col = (2 * b + i) * 256 + u * 128
-                        nc.tensor.transpose(
-                            out=xt[:, (2 * i + u) * 128 : (2 * i + u + 1) * 128],
-                            in_=words[:, col : col + 128],
-                            identity=ident[:],
-                        )
-                nc.scalar.copy(
-                    out=g_words[:, b * 512 : (b + 1) * 512].rearrange("p (i r u) -> p i r u", i=2, u=2),
-                    in_=xt[:].rearrange("p (i u r) -> p i r u", i=2, u=2),
-                )
+            xt[c, b] = psum.tile([P, 512], F32, name="xt%d" % b, tag="xt%d" % b)
+            for i in range(2):
+                for u in range(2):
+                    col = (2 * b + i) * 256 + u * 128
+                    nc.tensor.transpose(
+                        out=xt[c, b][:, (2 * i + u) * 128 : (2 * i + u + 1) * 128],
+                        in_=words[:, col : col + 128],
+                        identity=ident[:],
+                    )
 
-        def count_partial(c):
-            partial[c] = psum.tile([P, 512], F32, name="pc", tag="pc", bufs=2)
-            for j in range(TPC):
+        def evacuate(c, b):
+            if b == 0:
+                grouped[c] = gp.tile([P, TPC * K], BF16, name="g", tag="g", align_bytes=64)
+            g_words = grouped[c][:].bitcast(F32)
+            nc.scalar.copy(
+                out=g_words[:, b * 512 : (b + 1) * 512].rearrange("p (i r u) -> p i r u", i=2, u=2),
+                in_=xt[c, b][:].rearrange("p (i u r) -> p i r u", i=2, u=2),
+            )
+
+        def count_partial(c, half):
+            if half == 0:
+                partial[c] = psum.tile([P, 512], F32, name="pc", tag="pc", bufs=2)
+            for j in range(4 * half, 4 * half + 4):
                 for h in range(4):
                     col = (h * TPC + j) * NONES
                     nc.tensor.matmul(
@@ -167,35 +173,32 @@ def tile_flagbagencoder_t_kernel(tc, flags_matrix, emb_weight, out):
                 out=codes[c][:].bitcast(FP8X4), scales=scales[c][:], in_=grouped[c][:]
             )
 
-        def multiply(c):
-            sums[c] = []
-            for h in range(TPC // 4):
-                mo = psum.tile([P, 512], F32, name="mo%d" % h, tag="mo%d" % h)
-                sums[c].append(mo)
-                for q in range(4):
-                    j = 4 * h + q
-                    nc.tensor.matmul_mx(
-                        out=mo[:, q * D : (q + 1) * D],
-                        lhsT=codes[c][:, j * P : (j + 1) * P].bitcast(FP8X4),
-                        lhsT_scale=scales[c][:, j * P : (j + 1) * P],
-                        rhs=w_codes[:].bitcast(FP8X4),
-                        rhs_scale=w_scales[:],
-                        start=True,
-                        stop=True,
-                    )
+        def multiply(c, h):
+            sums[c, h] = psum.tile([P, 512], F32, name="mo%d" % h, tag="mo%d" % h)
+            for q in range(4):
+                j = 4 * h + q
+                nc.tensor.matmul_mx(
+                    out=sums[c, h][:, q * D : (q + 1) * D],
+                    lhsT=codes[c][:, j * P : (j + 1) * P].bitcast(FP8X4),
+                    lhsT_scale=scales[c][:, j * P : (j + 1) * P],
+                    rhs=w_codes[:].bitcast(FP8X4),
+                    rhs_scale=w_scales[:],
+                    start=True,
+                    stop=True,
+                )
 
         def finish(c):
             ot = op.tile([P, TPC * D], F32, name="ot", tag="ot")
             for j in range(4):
                 nc.scalar.activation(
                     out=ot[:, j * D : (j + 1) * D],
-                    in_=sums[c][0][:, j * D : (j + 1) * D],
+                    in_=sums[c, 0][:, j * D : (j + 1) * D],
                     func=ACT.Copy,
                     scale=rc[:, c * TPC + j : c * TPC + j + 1],
                 )
             nc.vector.tensor_tensor(
                 out=ot[:, 4 * D : 8 * D].rearrange("p (q d) -> p q d", d=D),
-                in0=sums[c][1][:].rearrange("p (q d) -> p q d", d=D),
+                in0=sums[c, 1][:].rearrange("p (q d) -> p q d", d=D),
                 in1=rc[:, c * TPC + 4 : c * TPC + 8].unsqueeze(2).to_broadcast([P, 4, D]),
                 op=ALU.mult,
             )
@@ -204,23 +207,35 @@ def tile_flagbagencoder_t_kernel(tc, flags_matrix, emb_weight, out):
                 in_=ot[:].rearrange("p (j d) -> p j d", d=D),
             )
 
+        nc.vector.memset(warm_in[:], 0.0)
+        nc.scalar.activation(out=warm_out[:], in_=warm_in[:], func=ACT.Copy, scale=1.0)
+        compare(0)
+        constants()
+        compare(1)
+        for b in range(4):
+            transpose(0, b)
+
         for k in range(NCH + 2):
             if k + PF < NCH:
                 load(k + PF)
-            if 0 <= k - 2:
-                count_partial_out(k - 2)
-                quantise(k - 2)
-            if 0 <= k - 1 < NCH:
-                transpose_evacuate(k - 1)
-            if 0 <= k - 2:
-                count_total(k - 2)
-                multiply(k - 2)
-            if k < NCH:
-                compare(k)
-            if k == 0:
-                constants()
+            for half in range(2):
+                if 0 <= k - 2:
+                    multiply(k - 2, half)
+                    if half == 0:
+                        count_total(k - 2)
+                if 0 <= k - 1 < NCH:
+                    count_partial(k - 1, half)
+                    if half == 0:
+                        quantise(k - 1)
+                if k < NCH:
+                    for b in (2 * half, 2 * half + 1):
+                        evacuate(k, b)
+                        if k + 1 < NCH:
+                            transpose(k + 1, b)
+            if k + 2 < NCH:
+                compare(k + 2)
             if 0 <= k - 2:
                 reciprocal(k - 2)
                 finish(k - 2)
             if 0 <= k - 1 < NCH:
-                count_partial(k - 1)
+                count_partial_out(k - 1)

@@ -82,6 +82,9 @@ def tile_flagbagencoder_t_kernel(tc, flags_matrix, emb_weight, out):
         sel = const.tile([P, 4 * P], BF16, name="sel")
         warm_in = const.tile([P, 8], F32, name="warm_in")
         warm_out = const.tile([P, 8], F32, name="warm_out")
+        zero_values = const.tile([P, 2048], BF16, name="zero_values", align_bytes=64)
+        zero_codes = const.tile([P, 512], U32, name="zero_codes", align_bytes=64)
+        zero_scales = const.tile([P, 512], U8, name="zero_scales", align_bytes=64)
 
         def constants():
             nc.vector.memset(ones[:], 1.0)
@@ -174,7 +177,8 @@ def tile_flagbagencoder_t_kernel(tc, flags_matrix, emb_weight, out):
             )
 
         def multiply(c, h):
-            sums[c, h] = psum.tile([P, 512], F32, name="mo%d" % h, tag="mo%d" % h)
+            tag = "xt%d" % h if c == NCH - 1 else "mo%d" % h
+            sums[c, h] = psum.tile([P, 512], F32, name=tag, tag=tag)
             for q in range(4):
                 j = 4 * h + q
                 nc.tensor.matmul_mx(
@@ -207,31 +211,51 @@ def tile_flagbagencoder_t_kernel(tc, flags_matrix, emb_weight, out):
                 in_=ot[:].rearrange("p (j d) -> p j d", d=D),
             )
 
+        def idle_passes(n):
+            for i in range(n):
+                nc.tensor.matmul_mx(
+                    out=junk[:],
+                    lhsT=zero_codes[:, 0:P].bitcast(FP8X4),
+                    lhsT_scale=zero_scales[:, 0:P],
+                    rhs=zero_codes[:].bitcast(FP8X4),
+                    rhs_scale=zero_scales[:],
+                    start=True,
+                    stop=True,
+                )
+
+        nc.vector.memset(zero_values[:].bitcast(I32), 0)
+        nc.vector.quantize_mx(
+            out=zero_codes[:].bitcast(FP8X4), scales=zero_scales[:], in_=zero_values[:]
+        )
         nc.vector.memset(warm_in[:], 0.0)
         nc.scalar.activation(out=warm_out[:], in_=warm_in[:], func=ACT.Copy, scale=1.0)
+        junk = psum.tile([P, 512], F32, name="junk", tag="mo0")
+        idle_passes(6)
         compare(0)
         constants()
         compare(1)
         for b in range(4):
             transpose(0, b)
+        idle_passes(2)
 
         for k in range(NCH + 2):
             if k + PF < NCH:
                 load(k + PF)
-            for half in range(2):
-                if 0 <= k - 2:
-                    multiply(k - 2, half)
-                    if half == 0:
-                        count_total(k - 2)
-                if 0 <= k - 1 < NCH:
-                    count_partial(k - 1, half)
-                    if half == 0:
-                        quantise(k - 1)
-                if k < NCH:
-                    for b in (2 * half, 2 * half + 1):
-                        evacuate(k, b)
-                        if k + 1 < NCH:
-                            transpose(k + 1, b)
+            if 0 <= k - 2:
+                multiply(k - 2, 0)
+                multiply(k - 2, 1)
+                count_total(k - 2)
+            if 0 <= k - 1 < NCH:
+                count_partial(k - 1, 0)
+                count_partial(k - 1, 1)
+                quantise(k - 1)
+            if k < NCH:
+                for b in range(4):
+                    evacuate(k, b)
+                    if k + 1 < NCH:
+                        transpose(k + 1, b)
+            if k < 2:
+                idle_passes(2)
             if k + 2 < NCH:
                 compare(k + 2)
             if 0 <= k - 2:

@@ -48,6 +48,7 @@ def tile_flagbagencoder_t_kernel(tc, flags_matrix, emb_weight, out):
         partial = {}
         partial_sb = {}
         xt = {}
+        scaled = {}
 
         w_raw = const.tile([P, 4, D], BF16, name="w_raw")
         nc.scalar.dma_start(
@@ -55,14 +56,12 @@ def tile_flagbagencoder_t_kernel(tc, flags_matrix, emb_weight, out):
             in_=emb_weight.rearrange("(u p e) d -> p u e d", u=2, e=2),
         )
 
-        def pieces_of(c):
-            return 4 if c == 0 else 1
-
         def load(c):
             fl[c] = flp.tile([P, TPC * K], BF16, name="fl", tag="fl")
             view = fl[c][:].rearrange("p (j k) -> p j k", k=K)
-            step = TPC // pieces_of(c)
-            for s in range(pieces_of(c)):
+            pieces = 4 if c == 0 else 1
+            step = TPC // pieces
+            for s in range(pieces):
                 nc.sync.dma_start(
                     out=view[:, s * step : (s + 1) * step, :],
                     in_=flags_v[:, c * TPC + s * step : c * TPC + (s + 1) * step, :],
@@ -101,16 +100,15 @@ def tile_flagbagencoder_t_kernel(tc, flags_matrix, emb_weight, out):
             for h in range(4):
                 nc.vector.tensor_copy(out=sel[:, h * P + 32 * h : h * P + 32 * h + 32], in_=fold[:])
 
-        def compare(c):
-            width = TPC * K // pieces_of(c)
-            for s in range(pieces_of(c)):
-                nc.vector.tensor_scalar(
-                    out=fl[c][:, s * width : (s + 1) * width],
-                    in0=fl[c][:, s * width : (s + 1) * width],
-                    scalar1=0.5,
-                    scalar2=None,
-                    op0=ALU.is_gt,
-                )
+        def compare(c, s, pieces):
+            width = TPC * K // pieces
+            nc.vector.tensor_scalar(
+                out=fl[c][:, s * width : (s + 1) * width],
+                in0=fl[c][:, s * width : (s + 1) * width],
+                scalar1=0.5,
+                scalar2=None,
+                op0=ALU.is_gt,
+            )
 
         def transpose(c, b):
             words = fl[c][:].bitcast(F32)
@@ -133,10 +131,10 @@ def tile_flagbagencoder_t_kernel(tc, flags_matrix, emb_weight, out):
                 in_=xt[c, b][:].rearrange("p (i u r) -> p i r u", i=2, u=2),
             )
 
-        def count_partial(c, half):
-            if half == 0:
+        def count_partial(c, tiles):
+            if tiles[0] == 0:
                 partial[c] = psum.tile([P, 512], F32, name="pc", tag="pc", bufs=2)
-            for j in range(4 * half, 4 * half + 4):
+            for j in tiles:
                 for h in range(4):
                     col = (h * TPC + j) * NONES
                     nc.tensor.matmul(
@@ -176,9 +174,21 @@ def tile_flagbagencoder_t_kernel(tc, flags_matrix, emb_weight, out):
                 out=codes[c][:].bitcast(FP8X4), scales=scales[c][:], in_=grouped[c][:]
             )
 
-        def multiply(c, h):
-            tag = "xt%d" % h if c == NCH - 1 else "mo%d" % h
-            sums[c, h] = psum.tile([P, 512], F32, name=tag, tag=tag)
+        def idle_passes(bank, n):
+            for i in range(n):
+                nc.tensor.matmul_mx(
+                    out=bank[:],
+                    lhsT=zero_codes[:, 0:P].bitcast(FP8X4),
+                    lhsT_scale=zero_scales[:, 0:P],
+                    rhs=zero_codes[:].bitcast(FP8X4),
+                    rhs_scale=zero_scales[:],
+                    start=True,
+                    stop=True,
+                )
+
+        def multiply(c, h, lead):
+            sums[c, h] = psum.tile([P, 512], F32, name="mo%d" % h, tag="mo%d" % h)
+            idle_passes(sums[c, h], lead)
             for q in range(4):
                 j = 4 * h + q
                 nc.tensor.matmul_mx(
@@ -191,37 +201,30 @@ def tile_flagbagencoder_t_kernel(tc, flags_matrix, emb_weight, out):
                     stop=True,
                 )
 
-        def finish(c):
-            ot = op.tile([P, TPC * D], F32, name="ot", tag="ot")
+        def scale_on_scalar(c):
+            scaled[c] = op.tile([P, TPC * D], F32, name="ot", tag="ot")
             for j in range(4):
                 nc.scalar.activation(
-                    out=ot[:, j * D : (j + 1) * D],
+                    out=scaled[c][:, j * D : (j + 1) * D],
                     in_=sums[c, 0][:, j * D : (j + 1) * D],
                     func=ACT.Copy,
                     scale=rc[:, c * TPC + j : c * TPC + j + 1],
                 )
+
+        def scale_on_vector_and_store(c):
             nc.vector.tensor_tensor(
-                out=ot[:, 4 * D : 8 * D].rearrange("p (q d) -> p q d", d=D),
+                out=scaled[c][:, 4 * D : 8 * D].rearrange("p (q d) -> p q d", d=D),
                 in0=sums[c, 1][:].rearrange("p (q d) -> p q d", d=D),
                 in1=rc[:, c * TPC + 4 : c * TPC + 8].unsqueeze(2).to_broadcast([P, 4, D]),
                 op=ALU.mult,
             )
             nc.sync.dma_start(
                 out=out_v[:, c * TPC : (c + 1) * TPC, :],
-                in_=ot[:].rearrange("p (j d) -> p j d", d=D),
+                in_=scaled[c][:].rearrange("p (j d) -> p j d", d=D),
             )
 
-        def idle_passes(n):
-            for i in range(n):
-                nc.tensor.matmul_mx(
-                    out=junk[:],
-                    lhsT=zero_codes[:, 0:P].bitcast(FP8X4),
-                    lhsT_scale=zero_scales[:, 0:P],
-                    rhs=zero_codes[:].bitcast(FP8X4),
-                    rhs_scale=zero_scales[:],
-                    start=True,
-                    stop=True,
-                )
+        def live(c):
+            return 0 <= c < NCH
 
         nc.vector.memset(zero_values[:].bitcast(I32), 0)
         nc.vector.quantize_mx(
@@ -230,36 +233,56 @@ def tile_flagbagencoder_t_kernel(tc, flags_matrix, emb_weight, out):
         nc.vector.memset(warm_in[:], 0.0)
         nc.scalar.activation(out=warm_out[:], in_=warm_in[:], func=ACT.Copy, scale=1.0)
         junk = psum.tile([P, 512], F32, name="junk", tag="mo0")
-        idle_passes(6)
-        compare(0)
+        idle_passes(junk, 6)
+        for s in range(4):
+            compare(0, s, 4)
         constants()
-        compare(1)
+        compare(1, 0, 2)
+        compare(1, 1, 2)
         for b in range(4):
             transpose(0, b)
-        idle_passes(2)
 
-        for k in range(NCH + 2):
+        for k in range(NCH + 3):
+            lead = 1 if k < NCH else 0
             if k + PF < NCH:
                 load(k + PF)
-            if 0 <= k - 2:
-                multiply(k - 2, 0)
-                multiply(k - 2, 1)
-                count_total(k - 2)
-            if 0 <= k - 1 < NCH:
-                count_partial(k - 1, 0)
-                count_partial(k - 1, 1)
+            if live(k - 3):
+                multiply(k - 3, 1, lead)
+            elif k < 3:
+                idle_passes(junk, 2)
+            if live(k - 1):
+                count_partial(k - 1, (0, 1))
                 quantise(k - 1)
-            if k < NCH:
-                for b in range(4):
+            if live(k - 2):
+                count_partial_out(k - 2)
+            if live(k - 3):
+                scale_on_vector_and_store(k - 3)
+            if live(k):
+                for b in (0, 1):
                     evacuate(k, b)
-                    if k + 1 < NCH:
+                    if live(k + 1):
                         transpose(k + 1, b)
-            if k < 2:
-                idle_passes(2)
-            if k + 2 < NCH:
-                compare(k + 2)
-            if 0 <= k - 2:
+            if live(k - 1):
+                count_partial(k - 1, (2, 3))
+            if live(k - 2):
+                count_total(k - 2)
+                multiply(k - 2, 0, lead)
+            elif k < 2:
+                idle_passes(junk, 2)
+            if live(k + 2):
+                compare(k + 2, 0, 2)
+            if live(k - 2):
                 reciprocal(k - 2)
-                finish(k - 2)
-            if 0 <= k - 1 < NCH:
-                count_partial_out(k - 1)
+            if live(k + 2):
+                compare(k + 2, 1, 2)
+            if live(k - 1):
+                count_partial(k - 1, (4, 5))
+            if live(k):
+                for b in (2, 3):
+                    evacuate(k, b)
+                    if live(k + 1):
+                        transpose(k + 1, b)
+            if live(k - 1):
+                count_partial(k - 1, (6, 7))
+            if live(k - 2):
+                scale_on_scalar(k - 2)

@@ -32,7 +32,8 @@ def tile_flagbagencoder_t_kernel(tc, flags_matrix, emb_weight, out):
 
     with ExitStack() as ctx:
         const = ctx.enter_context(tc.tile_pool(name="const", bufs=1))
-        flp = ctx.enter_context(tc.tile_pool(name="flp", bufs=NCH))
+        flp = ctx.enter_context(tc.tile_pool(name="flp", bufs=PF + 2))
+        mp = ctx.enter_context(tc.tile_pool(name="mp", bufs=3))
         gp = ctx.enter_context(tc.tile_pool(name="gp", bufs=3))
         cp = ctx.enter_context(tc.tile_pool(name="cp", bufs=3))
         op = ctx.enter_context(tc.tile_pool(name="op", bufs=6))
@@ -48,7 +49,7 @@ def tile_flagbagencoder_t_kernel(tc, flags_matrix, emb_weight, out):
         partial = {}
         partial_sb = {}
         xt = {}
-        scaled = {}
+        mask = {}
 
         w_raw = const.tile([P, 4, D], BF16, name="w_raw")
         nc.scalar.dma_start(
@@ -79,8 +80,6 @@ def tile_flagbagencoder_t_kernel(tc, flags_matrix, emb_weight, out):
         ones = const.tile([P, 16], BF16, name="ones")
         fold = const.tile([P, 32], F32, name="fold")
         sel = const.tile([P, 4 * P], BF16, name="sel")
-        warm_in = const.tile([P, 8], F32, name="warm_in")
-        warm_out = const.tile([P, 8], F32, name="warm_out")
         zero_values = const.tile([P, 2048], BF16, name="zero_values", align_bytes=64)
         zero_codes = const.tile([P, 512], U32, name="zero_codes", align_bytes=64)
         zero_scales = const.tile([P, 512], U8, name="zero_scales", align_bytes=64)
@@ -102,8 +101,10 @@ def tile_flagbagencoder_t_kernel(tc, flags_matrix, emb_weight, out):
 
         def compare(c, s, pieces):
             width = TPC * K // pieces
+            if s == 0:
+                mask[c] = mp.tile([P, TPC * K], BF16, name="mask", tag="mask")
             nc.vector.tensor_scalar(
-                out=fl[c][:, s * width : (s + 1) * width],
+                out=mask[c][:, s * width : (s + 1) * width],
                 in0=fl[c][:, s * width : (s + 1) * width],
                 scalar1=0.5,
                 scalar2=None,
@@ -111,7 +112,7 @@ def tile_flagbagencoder_t_kernel(tc, flags_matrix, emb_weight, out):
             )
 
         def transpose(c, b):
-            words = fl[c][:].bitcast(F32)
+            words = mask[c][:].bitcast(F32)
             xt[c, b] = psum.tile([P, 512], F32, name="xt%d" % b, tag="xt%d" % b)
             for i in range(2):
                 for u in range(2):
@@ -147,7 +148,7 @@ def tile_flagbagencoder_t_kernel(tc, flags_matrix, emb_weight, out):
 
         def count_partial_out(c):
             partial_sb[c] = small.tile([P, NB], BF16, name="p1", tag="p1")
-            nc.vector.tensor_copy(
+            nc.scalar.copy(
                 out=partial_sb[c][:],
                 in_=partial[c][:, 0 : NB * NONES].rearrange("p (b n) -> p b n", n=NONES)[:, :, 0],
             )
@@ -201,26 +202,18 @@ def tile_flagbagencoder_t_kernel(tc, flags_matrix, emb_weight, out):
                     stop=True,
                 )
 
-        def scale_on_scalar(c):
-            scaled[c] = op.tile([P, TPC * D], F32, name="ot", tag="ot")
-            for j in range(4):
-                nc.scalar.activation(
-                    out=scaled[c][:, j * D : (j + 1) * D],
-                    in_=sums[c, 0][:, j * D : (j + 1) * D],
-                    func=ACT.Copy,
-                    scale=rc[:, c * TPC + j : c * TPC + j + 1],
+        def scale_and_store(c):
+            scaled = op.tile([P, TPC * D], F32, name="ot", tag="ot")
+            for h in range(2):
+                nc.vector.tensor_tensor(
+                    out=scaled[:, 4 * h * D : 4 * (h + 1) * D].rearrange("p (q d) -> p q d", d=D),
+                    in0=sums[c, h][:].rearrange("p (q d) -> p q d", d=D),
+                    in1=rc[:, c * TPC + 4 * h : c * TPC + 4 * h + 4].unsqueeze(2).to_broadcast([P, 4, D]),
+                    op=ALU.mult,
                 )
-
-        def scale_on_vector_and_store(c):
-            nc.vector.tensor_tensor(
-                out=scaled[c][:, 4 * D : 8 * D].rearrange("p (q d) -> p q d", d=D),
-                in0=sums[c, 1][:].rearrange("p (q d) -> p q d", d=D),
-                in1=rc[:, c * TPC + 4 : c * TPC + 8].unsqueeze(2).to_broadcast([P, 4, D]),
-                op=ALU.mult,
-            )
             nc.sync.dma_start(
                 out=out_v[:, c * TPC : (c + 1) * TPC, :],
-                in_=scaled[c][:].rearrange("p (j d) -> p j d", d=D),
+                in_=scaled[:].rearrange("p (j d) -> p j d", d=D),
             )
 
         def live(c):
@@ -230,8 +223,6 @@ def tile_flagbagencoder_t_kernel(tc, flags_matrix, emb_weight, out):
         nc.vector.quantize_mx(
             out=zero_codes[:].bitcast(FP8X4), scales=zero_scales[:], in_=zero_values[:]
         )
-        nc.vector.memset(warm_in[:], 0.0)
-        nc.scalar.activation(out=warm_out[:], in_=warm_in[:], func=ACT.Copy, scale=1.0)
         junk = psum.tile([P, 512], F32, name="junk", tag="mo0")
         idle_passes(junk, 6)
         for s in range(4):
@@ -253,15 +244,15 @@ def tile_flagbagencoder_t_kernel(tc, flags_matrix, emb_weight, out):
             if live(k - 1):
                 count_partial(k - 1, (0, 1))
                 quantise(k - 1)
-            if live(k - 2):
-                count_partial_out(k - 2)
             if live(k - 3):
-                scale_on_vector_and_store(k - 3)
+                scale_and_store(k - 3)
             if live(k):
                 for b in (0, 1):
                     evacuate(k, b)
                     if live(k + 1):
                         transpose(k + 1, b)
+            if live(k - 2):
+                count_partial_out(k - 2)
             if live(k - 1):
                 count_partial(k - 1, (2, 3))
             if live(k - 2):
@@ -284,5 +275,3 @@ def tile_flagbagencoder_t_kernel(tc, flags_matrix, emb_weight, out):
                         transpose(k + 1, b)
             if live(k - 1):
                 count_partial(k - 1, (6, 7))
-            if live(k - 2):
-                scale_on_scalar(k - 2)

@@ -11,8 +11,10 @@ NT = T // P
 TPC = 8
 NCH = NT // TPC
 PF = 8
-NB = 4 * TPC
+NPE = 6
+NB = 4 * NPE
 NONES = 11
+WIDTHS = (512, 256, 256, 128)
 
 BF16 = mybir.dt.bfloat16
 F32 = mybir.dt.float32
@@ -74,23 +76,27 @@ def tile_flagbagencoder_t_kernel(tc, flags_matrix, emb_weight, out):
         ident = const.tile([P, P], F32, name="ident")
         make_identity(nc, ident[:])
         rc = const.tile([P, NT], F32, name="rc")
-        w_grouped = const.tile([P, D, 4], BF16, name="w_grouped", align_bytes=64)
-        w_codes = const.tile([P, D], U32, name="w_codes", align_bytes=64)
-        w_scales = const.tile([P, D], U8, name="w_scales", align_bytes=64)
+        w_grouped = const.tile([P, 4, D, 4], BF16, name="w_grouped", align_bytes=64)
+        w_codes = const.tile([P, 4 * D], U32, name="w_codes", align_bytes=64)
+        w_scales = const.tile([P, 4 * D], U8, name="w_scales", align_bytes=64)
         ones = const.tile([P, 16], BF16, name="ones")
         fold = const.tile([P, 32], F32, name="fold")
         sel = const.tile([P, 4 * P], BF16, name="sel")
+        counted = const.tile([P, NCH * (TPC - NPE)], F32, name="counted")
+        warm_in = const.tile([P, 8], F32, name="warm_in")
+        warm_out = const.tile([P, 8], F32, name="warm_out")
         zero_values = const.tile([P, 2048], BF16, name="zero_values", align_bytes=64)
         zero_codes = const.tile([P, 512], U32, name="zero_codes", align_bytes=64)
         zero_scales = const.tile([P, 512], U8, name="zero_scales", align_bytes=64)
 
         def constants():
             nc.vector.memset(ones[:], 1.0)
-            nc.vector.tensor_copy(out=w_grouped[:], in_=w_raw[:].rearrange("p t d -> p d t"))
+            for r in range(4):
+                nc.vector.tensor_copy(out=w_grouped[:, r, :, :], in_=w_raw[:].rearrange("p t d -> p d t"))
             nc.vector.quantize_mx(
                 out=w_codes[:].bitcast(FP8X4),
                 scales=w_scales[:],
-                in_=w_grouped[:].rearrange("p d t -> p (d t)"),
+                in_=w_grouped[:].rearrange("p r d t -> p (r d t)"),
             )
             nc.vector.tensor_reduce(
                 out=fold[:], in_=ident[:].rearrange("p (l t) -> p l t", t=4), axis=AX.X, op=ALU.add
@@ -137,7 +143,7 @@ def tile_flagbagencoder_t_kernel(tc, flags_matrix, emb_weight, out):
                 partial[c] = psum.tile([P, 512], F32, name="pc", tag="pc", bufs=2)
             for j in tiles:
                 for h in range(4):
-                    col = (h * TPC + j) * NONES
+                    col = (h * NPE + j) * NONES
                     nc.tensor.matmul(
                         out=partial[c][:, col : col + NONES],
                         lhsT=grouped[c][:, (4 * j + h) * P : (4 * j + h + 1) * P],
@@ -145,6 +151,17 @@ def tile_flagbagencoder_t_kernel(tc, flags_matrix, emb_weight, out):
                         start=True,
                         stop=True,
                     )
+
+        def count_on_scalar(c):
+            for j in range(NPE, TPC):
+                unused = small.tile([P, K], BF16, name="unused", tag="unused", bufs=2)
+                col = c * (TPC - NPE) + j - NPE
+                nc.scalar.activation(
+                    out=unused[:],
+                    in_=mask[c][:, j * K : (j + 1) * K],
+                    func=ACT.Copy,
+                    accum_out=counted[:, col : col + 1],
+                )
 
         def count_partial_out(c):
             partial_sb[c] = small.tile([P, NB], BF16, name="p1", tag="p1")
@@ -156,16 +173,21 @@ def tile_flagbagencoder_t_kernel(tc, flags_matrix, emb_weight, out):
         def count_total(c):
             for h in range(4):
                 nc.tensor.matmul(
-                    out=partial[c][:, 504:512],
+                    out=partial[c][:, 504 : 504 + NPE],
                     lhsT=sel[:, h * P : (h + 1) * P],
-                    rhs=partial_sb[c][:, h * TPC : (h + 1) * TPC],
+                    rhs=partial_sb[c][:, h * NPE : (h + 1) * NPE],
                     start=(h == 0),
                     stop=(h == 3),
                 )
 
         def reciprocal(c):
             cm = small.tile([P, TPC], F32, name="cm", tag="cm")
-            nc.vector.tensor_scalar_max(out=cm[:], in0=partial[c][:, 504:512], scalar1=1.0)
+            nc.vector.tensor_scalar_max(out=cm[:, 0:NPE], in0=partial[c][:, 504 : 504 + NPE], scalar1=1.0)
+            nc.vector.tensor_scalar_max(
+                out=cm[:, NPE:TPC],
+                in0=counted[:, c * (TPC - NPE) : (c + 1) * (TPC - NPE)],
+                scalar1=1.0,
+            )
             nc.vector.reciprocal(out=rc[:, c * TPC : (c + 1) * TPC], in_=cm[:])
 
         def quantise(c):
@@ -187,17 +209,17 @@ def tile_flagbagencoder_t_kernel(tc, flags_matrix, emb_weight, out):
                     stop=True,
                 )
 
-        def multiply(c, h, lead):
+        def multiply(c, h, wide):
             sums[c, h] = psum.tile([P, 512], F32, name="mo%d" % h, tag="mo%d" % h)
-            idle_passes(sums[c, h], lead)
             for q in range(4):
                 j = 4 * h + q
+                n = WIDTHS[q] if wide else D
                 nc.tensor.matmul_mx(
-                    out=sums[c, h][:, q * D : (q + 1) * D],
+                    out=sums[c, h][:, q * D : q * D + n],
                     lhsT=codes[c][:, j * P : (j + 1) * P].bitcast(FP8X4),
                     lhsT_scale=scales[c][:, j * P : (j + 1) * P],
-                    rhs=w_codes[:].bitcast(FP8X4),
-                    rhs_scale=w_scales[:],
+                    rhs=w_codes[:, 0:n].bitcast(FP8X4),
+                    rhs_scale=w_scales[:, 0:n],
                     start=True,
                     stop=True,
                 )
@@ -223,13 +245,14 @@ def tile_flagbagencoder_t_kernel(tc, flags_matrix, emb_weight, out):
         nc.vector.quantize_mx(
             out=zero_codes[:].bitcast(FP8X4), scales=zero_scales[:], in_=zero_values[:]
         )
+        nc.vector.memset(warm_in[:], 0.0)
+        nc.scalar.activation(out=warm_out[:], in_=warm_in[:], func=ACT.Copy, scale=1.0)
         junk = psum.tile([P, 512], F32, name="junk", tag="mo0")
         idle_passes(junk, 6)
         for s in range(4):
             compare(0, s, 4)
         constants()
-        compare(1, 0, 2)
-        compare(1, 1, 2)
+        compare(1, 0, 1)
         for b in range(4):
             transpose(0, b)
 
@@ -254,24 +277,26 @@ def tile_flagbagencoder_t_kernel(tc, flags_matrix, emb_weight, out):
             if live(k - 2):
                 count_partial_out(k - 2)
             if live(k - 1):
-                count_partial(k - 1, (2, 3))
+                count_partial(k - 1, (2,))
             if live(k - 2):
                 count_total(k - 2)
                 multiply(k - 2, 0, lead)
             elif k < 2:
                 idle_passes(junk, 2)
             if live(k + 2):
-                compare(k + 2, 0, 2)
+                compare(k + 2, 0, 1)
             if live(k - 2):
                 reciprocal(k - 2)
-            if live(k + 2):
-                compare(k + 2, 1, 2)
             if live(k - 1):
-                count_partial(k - 1, (4, 5))
+                count_partial(k - 1, (3, 4))
             if live(k):
                 for b in (2, 3):
                     evacuate(k, b)
                     if live(k + 1):
                         transpose(k + 1, b)
             if live(k - 1):
-                count_partial(k - 1, (6, 7))
+                count_partial(k - 1, (5,))
+            if k == 0:
+                count_on_scalar(0)
+            if live(k + 1):
+                count_on_scalar(k + 1)

from contextlib import ExitStack

import concourse.mybir as mybir
from concourse.masks import make_identity

T, K, D = 16384, 512, 128
FLOPS = 2 * T * K * D

P = 128
NT = T // P
TPC = 8
NCH = NT // TPC
PF = 8
NPE = 6
NB = 4 * NPE
NONES = 11
WIDTHS = (512, 256, 256, 128)

BF16 = mybir.dt.bfloat16
F32 = mybir.dt.float32
I32 = mybir.dt.int32
U32 = mybir.dt.uint32
U8 = mybir.dt.uint8
FP8X4 = mybir.dt.float8_e4m3fn_x4
ALU = mybir.AluOpType
ACT = mybir.ActivationFunctionType
AX = mybir.AxisListType


def tile_flagbagencoder_t_kernel(tc, flags_matrix, emb_weight, out):
    nc = tc.nc
    flags_v = flags_matrix.rearrange("(p j) k -> p j k", j=NT)
    out_v = out.rearrange("(p j) d -> p j d", j=NT)

    with ExitStack() as ctx:
        const = ctx.enter_context(tc.tile_pool(name="const", bufs=1))
        flp = ctx.enter_context(tc.tile_pool(name="flp", bufs=PF + 2))
        mp = ctx.enter_context(tc.tile_pool(name="mp", bufs=3))
        gp = ctx.enter_context(tc.tile_pool(name="gp", bufs=3))
        cp = ctx.enter_context(tc.tile_pool(name="cp", bufs=3))
        op = ctx.enter_context(tc.tile_pool(name="op", bufs=6))
        small = ctx.enter_context(tc.tile_pool(name="small", bufs=4))
        psum = ctx.enter_context(tc.psum_pool(name="psum", bufs=1))
        ctx.enter_context(tc.manual_schedule())

        fl = {}
        grouped = {}
        codes = {}
        scales = {}
        sums = {}
        partial = {}
        partial_sb = {}
        xt = {}
        mask = {}

        w_raw = const.tile([P, 4, D], BF16, name="w_raw")
        nc.scalar.dma_start(
            out=w_raw[:].rearrange("p (u e) d -> p u e d", u=2),
            in_=emb_weight.rearrange("(u p e) d -> p u e d", u=2, e=2),
        )

        def load(c):
            fl[c] = flp.tile([P, TPC * K], BF16, name="fl", tag="fl")
            view = fl[c][:].rearrange("p (j k) -> p j k", k=K)
            pieces = 4 if c == 0 else 1
            step = TPC // pieces
            for s in range(pieces):
                nc.sync.dma_start(
                    out=view[:, s * step : (s + 1) * step, :],
                    in_=flags_v[:, c * TPC + s * step : c * TPC + (s + 1) * step, :],
                )

        for c in range(PF):
            load(c)

        ident = const.tile([P, P], F32, name="ident")
        make_identity(nc, ident[:])
        rc = const.tile([P, NT], F32, name="rc")
        w_grouped = const.tile([P, 4, D, 4], BF16, name="w_grouped", align_bytes=64)
        w_codes = const.tile([P, 4 * D], U32, name="w_codes", align_bytes=64)
        w_scales = const.tile([P, 4 * D], U8, name="w_scales", align_bytes=64)
        ones = const.tile([P, 16], BF16, name="ones")
        fold = const.tile([P, 32], F32, name="fold")
        sel = const.tile([P, 4 * P], BF16, name="sel")
        counted = const.tile([P, NCH * (TPC - NPE)], F32, name="counted")
        warm_in = const.tile([P, 8], F32, name="warm_in")
        warm_out = const.tile([P, 8], F32, name="warm_out")
        zero_values = const.tile([P, 2048], BF16, name="zero_values", align_bytes=64)
        zero_codes = const.tile([P, 512], U32, name="zero_codes", align_bytes=64)
        zero_scales = const.tile([P, 512], U8, name="zero_scales", align_bytes=64)

        def constants():
            nc.vector.memset(ones[:], 1.0)
            for r in range(4):
                nc.vector.tensor_copy(out=w_grouped[:, r, :, :], in_=w_raw[:].rearrange("p t d -> p d t"))
            nc.vector.quantize_mx(
                out=w_codes[:].bitcast(FP8X4),
                scales=w_scales[:],
                in_=w_grouped[:].rearrange("p r d t -> p (r d t)"),
            )
            nc.vector.tensor_reduce(
                out=fold[:], in_=ident[:].rearrange("p (l t) -> p l t", t=4), axis=AX.X, op=ALU.add
            )
            nc.vector.memset(sel[:].bitcast(I32), 0)
            for h in range(4):
                nc.vector.tensor_copy(out=sel[:, h * P + 32 * h : h * P + 32 * h + 32], in_=fold[:])

        def compare(c, s, pieces):
            width = TPC * K // pieces
            if s == 0:
                mask[c] = mp.tile([P, TPC * K], BF16, name="mask", tag="mask")
            nc.vector.tensor_scalar(
                out=mask[c][:, s * width : (s + 1) * width],
                in0=fl[c][:, s * width : (s + 1) * width],
                scalar1=0.5,
                scalar2=None,
                op0=ALU.is_gt,
            )

        def transpose(c, b):
            words = mask[c][:].bitcast(F32)
            xt[c, b] = psum.tile([P, 512], F32, name="xt%d" % b, tag="xt%d" % b)
            for i in range(2):
                for u in range(2):
                    col = (2 * b + i) * 256 + u * 128
                    nc.tensor.transpose(
                        out=xt[c, b][:, (2 * i + u) * 128 : (2 * i + u + 1) * 128],
                        in_=words[:, col : col + 128],
                        identity=ident[:],
                    )

        def evacuate(c, b):
            if b == 0:
                grouped[c] = gp.tile([P, TPC * K], BF16, name="g", tag="g", align_bytes=64)
            g_words = grouped[c][:].bitcast(F32)
            nc.scalar.copy(
                out=g_words[:, b * 512 : (b + 1) * 512].rearrange("p (i r u) -> p i r u", i=2, u=2),
                in_=xt[c, b][:].rearrange("p (i u r) -> p i r u", i=2, u=2),
            )

        def count_partial(c, tiles):
            if tiles[0] == 0:
                partial[c] = psum.tile([P, 512], F32, name="pc", tag="pc", bufs=2)
            for j in tiles:
                for h in range(4):
                    col = (h * NPE + j) * NONES
                    nc.tensor.matmul(
                        out=partial[c][:, col : col + NONES],
                        lhsT=grouped[c][:, (4 * j + h) * P : (4 * j + h + 1) * P],
                        rhs=ones[:, 0:NONES],
                        start=True,
                        stop=True,
                    )

        def count_on_scalar(c):
            for j in range(NPE, TPC):
                unused = small.tile([P, K], BF16, name="unused", tag="unused", bufs=2)
                col = c * (TPC - NPE) + j - NPE
                nc.scalar.activation(
                    out=unused[:],
                    in_=mask[c][:, j * K : (j + 1) * K],
                    func=ACT.Copy,
                    accum_out=counted[:, col : col + 1],
                )

        def count_partial_out(c):
            partial_sb[c] = small.tile([P, NB], BF16, name="p1", tag="p1")
            nc.scalar.copy(
                out=partial_sb[c][:],
                in_=partial[c][:, 0 : NB * NONES].rearrange("p (b n) -> p b n", n=NONES)[:, :, 0],
            )

        def count_total(c):
            for h in range(4):
                nc.tensor.matmul(
                    out=partial[c][:, 504 : 504 + NPE],
                    lhsT=sel[:, h * P : (h + 1) * P],
                    rhs=partial_sb[c][:, h * NPE : (h + 1) * NPE],
                    start=(h == 0),
                    stop=(h == 3),
                )

        def reciprocal(c):
            cm = small.tile([P, TPC], F32, name="cm", tag="cm")
            nc.vector.tensor_scalar_max(out=cm[:, 0:NPE], in0=partial[c][:, 504 : 504 + NPE], scalar1=1.0)
            nc.vector.tensor_scalar_max(
                out=cm[:, NPE:TPC],
                in0=counted[:, c * (TPC - NPE) : (c + 1) * (TPC - NPE)],
                scalar1=1.0,
            )
            nc.vector.reciprocal(out=rc[:, c * TPC : (c + 1) * TPC], in_=cm[:])

        def quantise(c):
            codes[c] = cp.tile([P, TPC * P], U32, name="codes", tag="codes", align_bytes=64)
            scales[c] = cp.tile([P, TPC * P], U8, name="scl", tag="scl", align_bytes=64)
            nc.vector.quantize_mx(
                out=codes[c][:].bitcast(FP8X4), scales=scales[c][:], in_=grouped[c][:]
            )

        def idle_passes(bank, n):
            for i in range(n):
                nc.tensor.matmul_mx(
                    out=bank[:],
                    lhsT=zero_codes[:, 0:P].bitcast(FP8X4),
                    lhsT_scale=zero_scales[:, 0:P],
                    rhs=zero_codes[:].bitcast(FP8X4),
                    rhs_scale=zero_scales[:],
                    start=True,
                    stop=True,
                )

        def multiply(c, h, wide):
            sums[c, h] = psum.tile([P, 512], F32, name="mo%d" % h, tag="mo%d" % h)
            for q in range(4):
                j = 4 * h + q
                n = WIDTHS[q] if wide else D
                nc.tensor.matmul_mx(
                    out=sums[c, h][:, q * D : q * D + n],
                    lhsT=codes[c][:, j * P : (j + 1) * P].bitcast(FP8X4),
                    lhsT_scale=scales[c][:, j * P : (j + 1) * P],
                    rhs=w_codes[:, 0:n].bitcast(FP8X4),
                    rhs_scale=w_scales[:, 0:n],
                    start=True,
                    stop=True,
                )

        def scale_and_store(c):
            scaled = op.tile([P, TPC * D], F32, name="ot", tag="ot")
            for h in range(2):
                nc.vector.tensor_tensor(
                    out=scaled[:, 4 * h * D : 4 * (h + 1) * D].rearrange("p (q d) -> p q d", d=D),
                    in0=sums[c, h][:].rearrange("p (q d) -> p q d", d=D),
                    in1=rc[:, c * TPC + 4 * h : c * TPC + 4 * h + 4].unsqueeze(2).to_broadcast([P, 4, D]),
                    op=ALU.mult,
                )
            nc.sync.dma_start(
                out=out_v[:, c * TPC : (c + 1) * TPC, :],
                in_=scaled[:].rearrange("p (j d) -> p j d", d=D),
            )

        def live(c):
            return 0 <= c < NCH

        nc.vector.memset(zero_values[:].bitcast(I32), 0)
        nc.vector.quantize_mx(
            out=zero_codes[:].bitcast(FP8X4), scales=zero_scales[:], in_=zero_values[:]
        )
        nc.vector.memset(warm_in[:], 0.0)
        nc.scalar.activation(out=warm_out[:], in_=warm_in[:], func=ACT.Copy, scale=1.0)
        junk = psum.tile([P, 512], F32, name="junk", tag="mo0")
        idle_passes(junk, 6)
        for s in range(4):
            compare(0, s, 4)
        constants()
        compare(1, 0, 1)
        for b in range(4):
            transpose(0, b)

        for k in range(NCH + 3):
            lead = 1 if k < NCH else 0
            if k + PF < NCH:
                load(k + PF)
            if live(k - 3):
                multiply(k - 3, 1, lead)
            elif k < 3:
                idle_passes(junk, 2)
            if live(k - 1):
                count_partial(k - 1, (0, 1))
                quantise(k - 1)
            if live(k - 3):
                scale_and_store(k - 3)
            if live(k):
                for b in (0, 1):
                    evacuate(k, b)
                    if live(k + 1):
                        transpose(k + 1, b)
            if live(k - 2):
                count_partial_out(k - 2)
            if live(k - 1):
                count_partial(k - 1, (2,))
            if live(k - 2):
                count_total(k - 2)
                multiply(k - 2, 0, lead)
            elif k < 2:
                idle_passes(junk, 2)
            if live(k + 2):
                compare(k + 2, 0, 1)
            if live(k - 2):
                reciprocal(k - 2)
            if live(k - 1):
                count_partial(k - 1, (3, 4))
            if live(k):
                for b in (2, 3):
                    evacuate(k, b)
                    if live(k + 1):
                        transpose(k + 1, b)
            if live(k - 1):
                count_partial(k - 1, (5,))
            if k == 0:
                count_on_scalar(0)
            if live(k + 1):
                count_on_scalar(k + 1)
